import numpy as np
import ml_dtypes


def mxq(x, axis, fmt="e4m3"):
    dtype, down = {"e4m3": (ml_dtypes.float8_e4m3fn, 7), "e5m2": (ml_dtypes.float8_e5m2, 14)}[fmt]
    v = np.moveaxis(np.asarray(x, np.float32).astype(ml_dtypes.bfloat16).astype(np.float64), axis, -1)
    blocks = v.reshape(v.shape[:-1] + (-1, 32))
    amax = np.abs(blocks).max(-1, keepdims=True)
    byte = np.maximum(np.where(amax > 0, np.frexp(amax)[1] - 1 + 127, 0) - down, 1)
    scale = np.exp2(byte - 127.0)
    codes = (blocks / scale).astype(np.float32).astype(dtype).astype(np.float64)
    return np.moveaxis((codes * scale).reshape(v.shape), -1, axis)


WIDE = False


def mx_kscale(k):
    if not WIDE:
        return np.ones(k)
    levels = np.array([20, -20, 10, -10, 0])
    a = np.random.permutation(np.resize(levels, k // 512 * 4)).reshape(k // 512, 4)
    idx = np.arange(k)
    return np.exp2(a[idx // 512, idx % 128 // 32])


BF16 = ml_dtypes.bfloat16


def bf(x):
    return np.asarray(x, np.float32).astype(BF16)


def f64(x):
    return np.asarray(x).astype(np.float64)


N, F, H = 1536, 512, 512
SIG = 1.5
GS = 0.25


def elu(v):
    return np.where(v > 0.0, v, np.exp(np.minimum(v, 0.0)) - 1.0)


def log_softmax(v):
    z = v - v.max(axis=1, keepdims=True)
    return z - np.log(np.exp(z).sum(axis=1, keepdims=True))


def draw_adj():
    r = np.random.uniform(0.5, 1.5, (N, 1))
    return 2.0 * r * np.exp(SIG * np.random.standard_normal((N, N)) - 0.5 * SIG * SIG) / N


def setup_inputs():
    s = mx_kscale(N)[:, None]
    x = bf(elu(np.random.standard_normal((N, H)) * 0.9 + np.random.standard_normal(H) * 0.9))
    a0 = bf(draw_adj())
    w = bf(np.random.standard_normal((2 * H, H)) / np.sqrt(2 * H))
    b = bf(np.random.standard_normal(H) * 0.3)
    g = bf(np.random.standard_normal((N, H)) * np.exp2(np.random.randint(-12, 1, (N, 1))) * GS * s)
    xf, af, wf = f64(x), f64(a0), f64(w)
    deg = af.sum(axis=1, keepdims=True)
    agg = af @ xf
    nbar = agg / deg
    y = deg * (xf @ wf[:H]) + af @ (xf @ wf[H:]) + f64(b)
    p = np.exp(log_softmax(y))
    return {"x_gc2": x,
            "adj1": bf(af / s),
            "W3": w,
            "b3": b,
            "nbar": np.asarray(nbar, np.float32),
            "p": np.asarray(p, np.float32),
            "grad_out": g}


def reference(x_gc2, adj1, W3, b3, nbar, p, grad_out):
    g = f64(grad_out)
    deg = f64(adj1).sum(axis=1, keepdims=True)
    m = deg * np.concatenate([f64(x_gc2), f64(nbar)], axis=1)
    dy = g - f64(p) * g.sum(axis=1, keepdims=True)
    return mxq(m, 0, "e4m3").T @ mxq(dy, 0, "e5m2")

@@ -1,0 +1,141 @@
+from contextlib import ExitStack
+
+import concourse.mybir as mybir
+
+F32 = mybir.dt.float32
+BF16 = mybir.dt.bfloat16
+U32 = mybir.dt.uint32
+U8 = mybir.dt.uint8
+E4M3_X4 = mybir.dt.float8_e4m3fn_x4
+E5M2_X4 = mybir.dt.float8_e5m2_x4
+ALU = mybir.AluOpType
+ACT = mybir.ActivationFunctionType
+
+P = 128
+PACK = 4
+K_PASS = P * PACK
+NODES = 1536
+PASSES = NODES // K_PASS
+FEAT = 512
+M_TILE = 128
+HALF_TILES = FEAT // M_TILE
+RUN = 4
+SUM_PITCH = 8
+VECTOR_DEG_ROWS = 3
+
+FLOPS = 2 * NODES * (2 * FEAT) * FEAT
+BYTES = NODES * NODES * 2 + 2 * NODES * FEAT * 2 + 2 * NODES * FEAT * 4 + 2 * FEAT * FEAT * 4
+
+
+def pass_rows(dram, c):
+    return dram[c * K_PASS : (c + 1) * K_PASS, :].rearrange("(p j) w -> p j w", j=PACK)
+
+
+def regroup(nc, grouped, rows):
+    nc.vector.tensor_copy(
+        out=grouped[:].rearrange("p (c i) j -> p c j i", i=RUN),
+        in_=rows.rearrange("p j (c i) -> p c j i", i=RUN),
+    )
+
+
+def quantise(nc, codes, scales, grouped, x4_dtype):
+    nc.vector.quantize_mx(
+        out=codes[:].bitcast(x4_dtype),
+        scales=scales[:],
+        in_=grouped[:].rearrange("p w j -> p (w j)"),
+    )
+
+
+def tile_gcn_pc_v_kernel(tc, x_gc2, adj1, W3, b3, nbar, p, grad_out, out):
+    nc = tc.nc
+    with ExitStack() as ctx:
+        inputs = ctx.enter_context(tc.tile_pool(name="inputs", bufs=1))
+        sums = ctx.enter_context(tc.tile_pool(name="sums", bufs=1))
+        scrap = ctx.enter_context(tc.tile_pool(name="scrap", bufs=2))
+        work = ctx.enter_context(tc.tile_pool(name="work", bufs=3))
+        packed = ctx.enter_context(tc.tile_pool(name="packed", bufs=1))
+        results = ctx.enter_context(tc.tile_pool(name="results", bufs=1))
+        psum = ctx.enter_context(tc.psum_pool(name="psum", bufs=1))
+
+        g_sb, p_sb, adj_sb, x_sb, nbar_sb = [], [], [], [], []
+        for c in range(PASSES):
+            g_sb.append(inputs.tile([P, PACK, FEAT], BF16, name="g%d" % c))
+            p_sb.append(inputs.tile([P, PACK, FEAT], F32, name="p%d" % c))
+            adj_sb.append(inputs.tile([P, PACK, NODES], BF16, name="adj%d" % c))
+            x_sb.append(inputs.tile([P, PACK, FEAT], BF16, name="x%d" % c))
+            nbar_sb.append(inputs.tile([P, PACK, FEAT], F32, name="nbar%d" % c))
+            nc.sync.dma_start(out=g_sb[c][:], in_=pass_rows(grad_out, c))
+            nc.sync.dma_start(out=p_sb[c][:], in_=pass_rows(p, c))
+            nc.sync.dma_start(out=adj_sb[c][:], in_=pass_rows(adj1, c))
+            nc.sync.dma_start(out=x_sb[c][:], in_=pass_rows(x_gc2, c))
+            nc.sync.dma_start(out=nbar_sb[c][:], in_=pass_rows(nbar, c))
+
+        acc = [psum.tile([M_TILE, FEAT], F32, name="acc%d" % t) for t in range(2 * HALF_TILES)]
+
+        for c in range(PASSES):
+            neg_gsum = sums.tile([P, PACK, SUM_PITCH], F32, name="neg_gsum%d" % c)
+            for j in range(PACK):
+                neg_g = scrap.tile([P, FEAT], BF16, tag="neg_g")
+                nc.scalar.activation(
+                    out=neg_g[:], in_=g_sb[c][:, j, :], func=ACT.Copy, scale=-1.0,
+                    accum_out=neg_gsum[:, j, 0:1],
+                )
+            dy_rows = work.tile([P, PACK, FEAT], BF16)
+            for j in range(PACK):
+                nc.vector.scalar_tensor_tensor(
+                    out=dy_rows[:, j, :], in0=p_sb[c][:, j, :], scalar=neg_gsum[:, j, 0:1],
+                    in1=g_sb[c][:, j, :], op0=ALU.mult, op1=ALU.add,
+                )
+            dy_grouped = work.tile([P, FEAT, PACK], BF16, align_bytes=64)
+            regroup(nc, dy_grouped, dy_rows[:])
+
+            deg = sums.tile([P, PACK, SUM_PITCH], F32, name="deg%d" % c)
+            for j in range(PACK):
+                if j < VECTOR_DEG_ROWS:
+                    adj_copy_v = scrap.tile([P, NODES], BF16, tag="adj_copy_v")
+                    nc.vector.tensor_scalar(
+                        out=adj_copy_v[:], in0=adj_sb[c][:, j, :], scalar1=1.0, scalar2=None,
+                        op0=ALU.mult, op1=ALU.add, accum_out=deg[:, j, 0:1],
+                    )
+                else:
+                    adj_copy_s = scrap.tile([P, NODES], BF16, tag="adj_copy_s")
+                    nc.scalar.activation(
+                        out=adj_copy_s[:], in_=adj_sb[c][:, j, :], func=ACT.Copy,
+                        accum_out=deg[:, j, 0:1],
+                    )
+
+            dy_codes = packed.tile([P, FEAT], U32, name="dy_codes%d" % c, align_bytes=64)
+            dy_scales = packed.tile([P, FEAT], U8, name="dy_scales%d" % c, align_bytes=64)
+            quantise(nc, dy_codes, dy_scales, dy_grouped, E5M2_X4)
+
+            for half, source in enumerate((x_sb[c], nbar_sb[c])):
+                m_rows = work.tile([P, PACK, FEAT], BF16)
+                for j in range(PACK):
+                    nc.scalar.activation(
+                        out=m_rows[:, j, :], in_=source[:, j, :], func=ACT.Copy,
+                        scale=deg[:, j, 0:1],
+                    )
+                m_grouped = work.tile([P, FEAT, PACK], BF16, align_bytes=64)
+                regroup(nc, m_grouped, m_rows[:])
+                m_codes = packed.tile([P, FEAT], U32, name="m_codes%d_%d" % (c, half), align_bytes=64)
+                m_scales = packed.tile([P, FEAT], U8, name="m_scales%d_%d" % (c, half), align_bytes=64)
+                quantise(nc, m_codes, m_scales, m_grouped, E4M3_X4)
+                for t in range(HALF_TILES):
+                    m_cols = slice(t * M_TILE, (t + 1) * M_TILE)
+                    nc.tensor.matmul_mx(
+                        out=acc[half * HALF_TILES + t][:],
+                        lhsT=m_codes[:, m_cols].bitcast(E4M3_X4),
+                        lhsT_scale=m_scales[:, m_cols],
+                        rhs=dy_codes[:].bitcast(E5M2_X4),
+                        rhs_scale=dy_scales[:],
+                        start=(c == 0),
+                        stop=(c == PASSES - 1),
+                    )
+
+        for t in range(2 * HALF_TILES):
+            out_sb = results.tile([M_TILE, FEAT], F32, name="out_sb%d" % t)
+            if t % 2 == 0:
+                nc.scalar.copy(out=out_sb[:], in_=acc[t][:])
+            else:
+                nc.vector.tensor_copy(out=out_sb[:], in_=acc[t][:])
+            nc.sync.dma_start(out=out[t * M_TILE : (t + 1) * M_TILE, :], in_=out_sb[:])

@@ -16,12 +16,13 @@ PACK = 4
 K_PASS = P * PACK
 NODES = 1536
 PASSES = NODES // K_PASS
+LAST = PASSES - 1
 FEAT = 512
 M_TILE = 128
-HALF_TILES = FEAT // M_TILE
 RUN = 4
 SUM_PITCH = 8
-VECTOR_DEG_ROWS = 3
+SCALAR_DEG_ROWS = 2
+LAST_NBAR_PIECES = 2
 
 FLOPS = 2 * NODES * (2 * FEAT) * FEAT
 BYTES = NODES * NODES * 2 + 2 * NODES * FEAT * 2 + 2 * NODES * FEAT * 4 + 2 * FEAT * FEAT * 4
@@ -31,111 +32,169 @@ def pass_rows(dram, c):
     return dram[c * K_PASS : (c + 1) * K_PASS, :].rearrange("(p j) w -> p j w", j=PACK)
 
 
-def regroup(nc, grouped, rows):
-    nc.vector.tensor_copy(
-        out=grouped[:].rearrange("p (c i) j -> p c j i", i=RUN),
-        in_=rows.rearrange("p j (c i) -> p c j i", i=RUN),
-    )
-
-
-def quantise(nc, codes, scales, grouped, x4_dtype):
-    nc.vector.quantize_mx(
-        out=codes[:].bitcast(x4_dtype),
-        scales=scales[:],
-        in_=grouped[:].rearrange("p w j -> p (w j)"),
-    )
-
-
 def tile_gcn_pc_v_kernel(tc, x_gc2, adj1, W3, b3, nbar, p, grad_out, out):
     nc = tc.nc
     with ExitStack() as ctx:
         inputs = ctx.enter_context(tc.tile_pool(name="inputs", bufs=1))
         sums = ctx.enter_context(tc.tile_pool(name="sums", bufs=1))
         scrap = ctx.enter_context(tc.tile_pool(name="scrap", bufs=2))
-        work = ctx.enter_context(tc.tile_pool(name="work", bufs=3))
+        work = ctx.enter_context(tc.tile_pool(name="work", bufs=2))
         packed = ctx.enter_context(tc.tile_pool(name="packed", bufs=1))
         results = ctx.enter_context(tc.tile_pool(name="results", bufs=1))
         psum = ctx.enter_context(tc.psum_pool(name="psum", bufs=1))
+        ctx.enter_context(tc.manual_schedule())
 
-        g_sb, p_sb, adj_sb, x_sb, nbar_sb = [], [], [], [], []
+        g_sb = [inputs.tile([P, PACK, FEAT], BF16, name="g%d" % c) for c in range(PASSES)]
+        p_sb = [inputs.tile([P, PACK, FEAT], F32, name="p%d" % c) for c in range(PASSES)]
+        adj_sb = [inputs.tile([P, PACK, NODES], BF16, name="adj%d" % c) for c in range(PASSES)]
+        x_sb = [inputs.tile([P, PACK, FEAT], BF16, name="x%d" % c) for c in range(PASSES)]
+        nbar_sb = [inputs.tile([P, PACK, FEAT], F32, name="nbar%d" % c) for c in range(PASSES)]
+        neg_gsum = [sums.tile([P, PACK, SUM_PITCH], F32, name="neg_gsum%d" % c) for c in range(PASSES)]
+        deg = [sums.tile([P, PACK, SUM_PITCH], F32, name="deg%d" % c) for c in range(PASSES)]
+        dy_codes = [packed.tile([P, FEAT], U32, name="dy_codes%d" % c, align_bytes=64) for c in range(PASSES)]
+        dy_scales = [packed.tile([P, FEAT], U8, name="dy_scales%d" % c, align_bytes=64) for c in range(PASSES)]
+        acc = [psum.tile([M_TILE, FEAT], F32, name="acc%d" % t) for t in range(2 * FEAT // M_TILE)]
+
+        def load(tile_sb, dram, c, pieces):
+            step = PACK // pieces
+            for j in range(0, PACK, step):
+                nc.sync.dma_start(out=tile_sb[c][:, j : j + step, :], in_=pass_rows(dram, c)[:, j : j + step, :])
+
+        def load_dy_inputs(c, pieces):
+            step = PACK // pieces
+            for j in range(0, PACK, step):
+                nc.sync.dma_start(out=g_sb[c][:, j : j + step, :], in_=pass_rows(grad_out, c)[:, j : j + step, :])
+                nc.sync.dma_start(out=p_sb[c][:, j : j + step, :], in_=pass_rows(p, c)[:, j : j + step, :])
+
+        load_dy_inputs(0, 2)
+        load(adj_sb, adj1, 0, 2)
         for c in range(PASSES):
-            g_sb.append(inputs.tile([P, PACK, FEAT], BF16, name="g%d" % c))
-            p_sb.append(inputs.tile([P, PACK, FEAT], F32, name="p%d" % c))
-            adj_sb.append(inputs.tile([P, PACK, NODES], BF16, name="adj%d" % c))
-            x_sb.append(inputs.tile([P, PACK, FEAT], BF16, name="x%d" % c))
-            nbar_sb.append(inputs.tile([P, PACK, FEAT], F32, name="nbar%d" % c))
-            nc.sync.dma_start(out=g_sb[c][:], in_=pass_rows(grad_out, c))
-            nc.sync.dma_start(out=p_sb[c][:], in_=pass_rows(p, c))
-            nc.sync.dma_start(out=adj_sb[c][:], in_=pass_rows(adj1, c))
-            nc.sync.dma_start(out=x_sb[c][:], in_=pass_rows(x_gc2, c))
-            nc.sync.dma_start(out=nbar_sb[c][:], in_=pass_rows(nbar, c))
+            if c < LAST:
+                load_dy_inputs(c + 1, 1)
+            load(x_sb, x_gc2, c, 1)
+            if c < LAST:
+                load(nbar_sb, nbar, c, 1)
+                load(adj_sb, adj1, c + 1, 2)
+        piece_cols = FEAT // LAST_NBAR_PIECES
+        for w in range(0, FEAT, piece_cols):
+            nc.sync.dma_start(out=nbar_sb[LAST][:, :, w : w + piece_cols], in_=pass_rows(nbar, LAST)[:, :, w : w + piece_cols])
 
-        acc = [psum.tile([M_TILE, FEAT], F32, name="acc%d" % t) for t in range(2 * HALF_TILES)]
-
-        for c in range(PASSES):
-            neg_gsum = sums.tile([P, PACK, SUM_PITCH], F32, name="neg_gsum%d" % c)
+        def sum_grad_rows(c):
             for j in range(PACK):
                 neg_g = scrap.tile([P, FEAT], BF16, tag="neg_g")
                 nc.scalar.activation(
                     out=neg_g[:], in_=g_sb[c][:, j, :], func=ACT.Copy, scale=-1.0,
-                    accum_out=neg_gsum[:, j, 0:1],
+                    accum_out=neg_gsum[c][:, j, 0:1],
                 )
-            dy_rows = work.tile([P, PACK, FEAT], BF16)
+
+        def dy_rows_of(c):
+            dy_rows = work.tile([P, PACK, FEAT], BF16, tag="dy_rows")
             for j in range(PACK):
                 nc.vector.scalar_tensor_tensor(
-                    out=dy_rows[:, j, :], in0=p_sb[c][:, j, :], scalar=neg_gsum[:, j, 0:1],
+                    out=dy_rows[:, j, :], in0=p_sb[c][:, j, :], scalar=neg_gsum[c][:, j, 0:1],
                     in1=g_sb[c][:, j, :], op0=ALU.mult, op1=ALU.add,
                 )
-            dy_grouped = work.tile([P, FEAT, PACK], BF16, align_bytes=64)
-            regroup(nc, dy_grouped, dy_rows[:])
+            return dy_rows
 
-            deg = sums.tile([P, PACK, SUM_PITCH], F32, name="deg%d" % c)
+        def sum_adj_rows(c):
             for j in range(PACK):
-                if j < VECTOR_DEG_ROWS:
-                    adj_copy_v = scrap.tile([P, NODES], BF16, tag="adj_copy_v")
-                    nc.vector.tensor_scalar(
-                        out=adj_copy_v[:], in0=adj_sb[c][:, j, :], scalar1=1.0, scalar2=None,
-                        op0=ALU.mult, op1=ALU.add, accum_out=deg[:, j, 0:1],
-                    )
-                else:
+                if j < SCALAR_DEG_ROWS:
                     adj_copy_s = scrap.tile([P, NODES], BF16, tag="adj_copy_s")
                     nc.scalar.activation(
                         out=adj_copy_s[:], in_=adj_sb[c][:, j, :], func=ACT.Copy,
-                        accum_out=deg[:, j, 0:1],
+                        accum_out=deg[c][:, j, 0:1],
+                    )
+                else:
+                    adj_copy_v = scrap.tile([P, NODES], BF16, tag="adj_copy_v")
+                    nc.vector.tensor_scalar(
+                        out=adj_copy_v[:], in0=adj_sb[c][:, j, :], scalar1=1.0, scalar2=None,
+                        op0=ALU.mult, op1=ALU.add, accum_out=deg[c][:, j, 0:1],
                     )
 
-            dy_codes = packed.tile([P, FEAT], U32, name="dy_codes%d" % c, align_bytes=64)
-            dy_scales = packed.tile([P, FEAT], U8, name="dy_scales%d" % c, align_bytes=64)
-            quantise(nc, dy_codes, dy_scales, dy_grouped, E5M2_X4)
+        def x_rows_of(c):
+            x_rows = work.tile([P, PACK, FEAT], BF16, tag="x_rows")
+            for j in range(PACK):
+                nc.vector.tensor_scalar(
+                    out=x_rows[:, j, :], in0=x_sb[c][:, j, :], scalar1=deg[c][:, j, 0:1], scalar2=None,
+                    op0=ALU.mult,
+                )
+            return x_rows
 
-            for half, source in enumerate((x_sb[c], nbar_sb[c])):
-                m_rows = work.tile([P, PACK, FEAT], BF16)
-                for j in range(PACK):
-                    nc.scalar.activation(
-                        out=m_rows[:, j, :], in_=source[:, j, :], func=ACT.Copy,
-                        scale=deg[:, j, 0:1],
-                    )
-                m_grouped = work.tile([P, FEAT, PACK], BF16, align_bytes=64)
-                regroup(nc, m_grouped, m_rows[:])
-                m_codes = packed.tile([P, FEAT], U32, name="m_codes%d_%d" % (c, half), align_bytes=64)
-                m_scales = packed.tile([P, FEAT], U8, name="m_scales%d_%d" % (c, half), align_bytes=64)
-                quantise(nc, m_codes, m_scales, m_grouped, E4M3_X4)
-                for t in range(HALF_TILES):
-                    m_cols = slice(t * M_TILE, (t + 1) * M_TILE)
-                    nc.tensor.matmul_mx(
-                        out=acc[half * HALF_TILES + t][:],
-                        lhsT=m_codes[:, m_cols].bitcast(E4M3_X4),
-                        lhsT_scale=m_scales[:, m_cols],
-                        rhs=dy_codes[:].bitcast(E5M2_X4),
-                        rhs_scale=dy_scales[:],
-                        start=(c == 0),
-                        stop=(c == PASSES - 1),
-                    )
+        def nbar_rows_of(c, w, cols):
+            n_rows = work.tile([P, PACK, cols], BF16, tag="n_rows")
+            for j in range(PACK):
+                nc.scalar.activation(
+                    out=n_rows[:, j, :], in_=nbar_sb[c][:, j, w : w + cols], func=ACT.Copy,
+                    scale=deg[c][:, j, 0:1],
+                )
+            return n_rows
 
-        for t in range(2 * HALF_TILES):
+        def regroup(rows, cols, tag):
+            grouped = work.tile([P, cols, PACK], BF16, tag=tag, align_bytes=64)
+            nc.vector.tensor_copy(
+                out=grouped[:].rearrange("p (c i) j -> p c j i", i=RUN),
+                in_=rows[:].rearrange("p j (c i) -> p c j i", i=RUN),
+            )
+            return grouped
+
+        def quantise_dy(c, grouped):
+            nc.vector.quantize_mx(
+                out=dy_codes[c][:].bitcast(E5M2_X4), scales=dy_scales[c][:],
+                in_=grouped[:].rearrange("p w j -> p (w j)"),
+            )
+
+        def quantise_m_and_multiply(c, grouped, first_row, cols):
+            m_codes = packed.tile([P, cols], U32, name="m_codes%d_%d" % (c, first_row), align_bytes=64)
+            m_scales = packed.tile([P, cols], U8, name="m_scales%d_%d" % (c, first_row), align_bytes=64)
+            nc.vector.quantize_mx(
+                out=m_codes[:].bitcast(E4M3_X4), scales=m_scales[:],
+                in_=grouped[:].rearrange("p w j -> p (w j)"),
+            )
+            for w in range(0, cols, M_TILE):
+                nc.tensor.matmul_mx(
+                    out=acc[(first_row + w) // M_TILE][:],
+                    lhsT=m_codes[:, w : w + M_TILE].bitcast(E4M3_X4),
+                    lhsT_scale=m_scales[:, w : w + M_TILE],
+                    rhs=dy_codes[c][:].bitcast(E5M2_X4),
+                    rhs_scale=dy_scales[c][:],
+                    start=(c == 0),
+                    stop=(c == LAST),
+                )
+
+        def store(t, engine_copy):
             out_sb = results.tile([M_TILE, FEAT], F32, name="out_sb%d" % t)
-            if t % 2 == 0:
-                nc.scalar.copy(out=out_sb[:], in_=acc[t][:])
-            else:
-                nc.vector.tensor_copy(out=out_sb[:], in_=acc[t][:])
+            engine_copy(out=out_sb[:], in_=acc[t][:])
             nc.sync.dma_start(out=out[t * M_TILE : (t + 1) * M_TILE, :], in_=out_sb[:])
+
+        sum_grad_rows(0)
+        dy_rows = dy_rows_of(0)
+        dy_grouped = regroup(dy_rows, FEAT, "dy_grouped")
+        sum_adj_rows(0)
+        quantise_dy(0, dy_grouped)
+        for c in range(LAST):
+            sum_grad_rows(c + 1)
+            dy_rows = dy_rows_of(c + 1)
+            x_rows = x_rows_of(c)
+            n_rows = nbar_rows_of(c, 0, FEAT)
+            dy_grouped = regroup(dy_rows, FEAT, "dy_grouped")
+            x_grouped = regroup(x_rows, FEAT, "x_grouped")
+            quantise_dy(c + 1, dy_grouped)
+            n_grouped = regroup(n_rows, FEAT, "n_grouped")
+            quantise_m_and_multiply(c, x_grouped, 0, FEAT)
+            sum_adj_rows(c + 1)
+            quantise_m_and_multiply(c, n_grouped, FEAT, FEAT)
+
+        x_rows = x_rows_of(LAST)
+        n_rows = [nbar_rows_of(LAST, w, piece_cols) for w in range(0, FEAT, piece_cols)]
+        x_grouped = regroup(x_rows, FEAT, "x_grouped")
+        n_grouped = regroup(n_rows[0], piece_cols, "n_grouped")
+        quantise_m_and_multiply(LAST, x_grouped, 0, FEAT)
+        for t in range(FEAT // M_TILE):
+            store(t, nc.scalar.copy)
+        for k in range(LAST_NBAR_PIECES):
+            this_grouped = n_grouped
+            if k + 1 < LAST_NBAR_PIECES:
+                n_grouped = regroup(n_rows[k + 1], piece_cols, "n_grouped")
+            quantise_m_and_multiply(LAST, this_grouped, FEAT + k * piece_cols, piece_cols)
+        for t in range(FEAT // M_TILE, 2 * FEAT // M_TILE):
+            store(t, nc.scalar.copy if t % 2 == 0 else nc.vector.tensor_copy)

@@ -1,6 +1,7 @@
 from contextlib import ExitStack
 
 import concourse.mybir as mybir
+from concourse.masks import make_identity
 
 F32 = mybir.dt.float32
 BF16 = mybir.dt.bfloat16
@@ -21,7 +22,10 @@ FEAT = 512
 M_TILE = 128
 RUN = 4
 SUM_PITCH = 8
-SCALAR_DEG_ROWS = 2
+FOLD_COLS = 128
+FOLDED_DEG_ROW = 0
+SCALAR_DEG_ROW = 1
+LENT_TILE = 7
 LAST_NBAR_PIECES = 2
 
 FLOPS = 2 * NODES * (2 * FEAT) * FEAT
@@ -53,7 +57,10 @@ def tile_gcn_pc_v_kernel(tc, x_gc2, adj1, W3, b3, nbar, p, grad_out, out):
         deg = [sums.tile([P, PACK, SUM_PITCH], F32, name="deg%d" % c) for c in range(PASSES)]
         dy_codes = [packed.tile([P, FEAT], U32, name="dy_codes%d" % c, align_bytes=64) for c in range(PASSES)]
         dy_scales = [packed.tile([P, FEAT], U8, name="dy_scales%d" % c, align_bytes=64) for c in range(PASSES)]
-        acc = [psum.tile([M_TILE, FEAT], F32, name="acc%d" % t) for t in range(2 * FEAT // M_TILE)]
+        acc = [psum.tile([M_TILE, FEAT], F32, name="acc%d" % t) for t in range(LENT_TILE)]
+        waiting = []
+        ident = sums.tile([P, P], BF16, name="ident")
+        make_identity(nc, ident[:])
 
         def load(tile_sb, dram, c, pieces):
             step = PACK // pieces
@@ -96,9 +103,26 @@ def tile_gcn_pc_v_kernel(tc, x_gc2, adj1, W3, b3, nbar, p, grad_out, out):
                 )
             return dy_rows
 
-        def sum_adj_rows(c):
+        def fold_adj_row(c):
+            fold = psum.tile([P, FOLD_COLS], F32, name="fold%d" % c, tag="lent_bank")
+            pieces = NODES // FOLD_COLS
+            for k in range(pieces):
+                nc.tensor.matmul(
+                    out=fold[:], lhsT=ident[:],
+                    rhs=adj_sb[c][:, FOLDED_DEG_ROW, k * FOLD_COLS : (k + 1) * FOLD_COLS],
+                    start=(k == 0), stop=(k == pieces - 1),
+                )
+            return fold
+
+        def sum_adj_rows(c, fold):
             for j in range(PACK):
-                if j < SCALAR_DEG_ROWS:
+                if j == FOLDED_DEG_ROW:
+                    fold_copy = scrap.tile([P, FOLD_COLS], BF16, tag="fold_copy")
+                    nc.scalar.activation(
+                        out=fold_copy[:], in_=fold[:], func=ACT.Copy,
+                        accum_out=deg[c][:, j, 0:1],
+                    )
+                elif j == SCALAR_DEG_ROW:
                     adj_copy_s = scrap.tile([P, NODES], BF16, tag="adj_copy_s")
                     nc.scalar.activation(
                         out=adj_copy_s[:], in_=adj_sb[c][:, j, :], func=ACT.Copy,
@@ -129,9 +153,9 @@ def tile_gcn_pc_v_kernel(tc, x_gc2, adj1, W3, b3, nbar, p, grad_out, out):
                 )
             return n_rows
 
-        def regroup(rows, cols, tag):
+        def regroup(rows, cols, tag, engine_copy):
             grouped = work.tile([P, cols, PACK], BF16, tag=tag, align_bytes=64)
-            nc.vector.tensor_copy(
+            engine_copy(
                 out=grouped[:].rearrange("p (c i) j -> p c j i", i=RUN),
                 in_=rows[:].rearrange("p j (c i) -> p c j i", i=RUN),
             )
@@ -151,15 +175,20 @@ def tile_gcn_pc_v_kernel(tc, x_gc2, adj1, W3, b3, nbar, p, grad_out, out):
                 in_=grouped[:].rearrange("p w j -> p (w j)"),
             )
             for w in range(0, cols, M_TILE):
+                waiting.append((c, (first_row + w) // M_TILE, m_codes[:, w : w + M_TILE], m_scales[:, w : w + M_TILE]))
+            held = [one for one in waiting if one[1] >= len(acc)]
+            for c_of, t, codes, scales in [one for one in waiting if one[1] < len(acc)]:
                 nc.tensor.matmul_mx(
-                    out=acc[(first_row + w) // M_TILE][:],
-                    lhsT=m_codes[:, w : w + M_TILE].bitcast(E4M3_X4),
-                    lhsT_scale=m_scales[:, w : w + M_TILE],
-                    rhs=dy_codes[c][:].bitcast(E5M2_X4),
-                    rhs_scale=dy_scales[c][:],
-                    start=(c == 0),
-                    stop=(c == LAST),
+                    out=acc[t][:],
+                    lhsT=codes.bitcast(E4M3_X4),
+                    lhsT_scale=scales,
+                    rhs=dy_codes[c_of][:].bitcast(E5M2_X4),
+                    rhs_scale=dy_scales[c_of][:],
+                    start=(c_of == 0),
+                    stop=(c_of == LAST),
                 )
+            waiting.clear()
+            waiting.extend(held)
 
         def store(t, engine_copy):
             out_sb = results.tile([M_TILE, FEAT], F32, name="out_sb%d" % t)
@@ -168,33 +197,36 @@ def tile_gcn_pc_v_kernel(tc, x_gc2, adj1, W3, b3, nbar, p, grad_out, out):
 
         sum_grad_rows(0)
         dy_rows = dy_rows_of(0)
-        dy_grouped = regroup(dy_rows, FEAT, "dy_grouped")
-        sum_adj_rows(0)
+        dy_grouped = regroup(dy_rows, FEAT, "dy_grouped", nc.vector.tensor_copy)
+        sum_adj_rows(0, fold_adj_row(0))
         quantise_dy(0, dy_grouped)
         for c in range(LAST):
+            fold = fold_adj_row(c + 1)
             sum_grad_rows(c + 1)
             dy_rows = dy_rows_of(c + 1)
             x_rows = x_rows_of(c)
             n_rows = nbar_rows_of(c, 0, FEAT)
-            dy_grouped = regroup(dy_rows, FEAT, "dy_grouped")
-            x_grouped = regroup(x_rows, FEAT, "x_grouped")
+            dy_grouped = regroup(dy_rows, FEAT, "dy_grouped", nc.vector.tensor_copy)
+            x_grouped = regroup(x_rows, FEAT, "x_grouped", nc.vector.tensor_copy)
+            n_grouped = regroup(n_rows, FEAT, "n_grouped", nc.scalar.copy)
             quantise_dy(c + 1, dy_grouped)
-            n_grouped = regroup(n_rows, FEAT, "n_grouped")
             quantise_m_and_multiply(c, x_grouped, 0, FEAT)
-            sum_adj_rows(c + 1)
+            sum_adj_rows(c + 1, fold)
+            if c + 1 == LAST:
+                acc.append(psum.tile([M_TILE, FEAT], F32, name="acc%d" % LENT_TILE, tag="lent_bank"))
             quantise_m_and_multiply(c, n_grouped, FEAT, FEAT)
 
         x_rows = x_rows_of(LAST)
         n_rows = [nbar_rows_of(LAST, w, piece_cols) for w in range(0, FEAT, piece_cols)]
-        x_grouped = regroup(x_rows, FEAT, "x_grouped")
-        n_grouped = regroup(n_rows[0], piece_cols, "n_grouped")
+        x_grouped = regroup(x_rows, FEAT, "x_grouped", nc.vector.tensor_copy)
+        n_grouped = regroup(n_rows[0], piece_cols, "n_grouped", nc.vector.tensor_copy)
         quantise_m_and_multiply(LAST, x_grouped, 0, FEAT)
         for t in range(FEAT // M_TILE):
             store(t, nc.scalar.copy)
         for k in range(LAST_NBAR_PIECES):
             this_grouped = n_grouped
             if k + 1 < LAST_NBAR_PIECES:
-                n_grouped = regroup(n_rows[k + 1], piece_cols, "n_grouped")
+                n_grouped = regroup(n_rows[k + 1], piece_cols, "n_grouped", nc.vector.tensor_copy)
             quantise_m_and_multiply(LAST, this_grouped, FEAT + k * piece_cols, piece_cols)
         for t in range(FEAT // M_TILE, 2 * FEAT // M_TILE):
             store(t, nc.scalar.copy if t % 2 == 0 else nc.vector.tensor_copy)

@@ -20,13 +20,16 @@ PASSES = NODES // K_PASS
 LAST = PASSES - 1
 FEAT = 512
 M_TILE = 128
+TILES = 2 * FEAT // M_TILE
 RUN = 4
 SUM_PITCH = 8
 FOLD_COLS = 128
-FOLDED_DEG_ROW = 0
-SCALAR_DEG_ROW = 1
-LENT_TILE = 7
-LAST_NBAR_PIECES = 2
+SCALAR_DEG_ROWS = (0, 1)
+FOLDED_DEG_ROW = 2
+VECTOR_DEG_ROW = 3
+LENT_TILE = TILES - 1
+LAST_X_PIECES = (256, 256)
+LAST_NBAR_PIECES = (256, 128, 128)
 
 FLOPS = 2 * NODES * (2 * FEAT) * FEAT
 BYTES = NODES * NODES * 2 + 2 * NODES * FEAT * 2 + 2 * NODES * FEAT * 4 + 2 * FEAT * FEAT * 4
@@ -62,29 +65,30 @@ def tile_gcn_pc_v_kernel(tc, x_gc2, adj1, W3, b3, nbar, p, grad_out, out):
         ident = sums.tile([P, P], BF16, name="ident")
         make_identity(nc, ident[:])
 
-        def load(tile_sb, dram, c, pieces):
-            step = PACK // pieces
-            for j in range(0, PACK, step):
-                nc.sync.dma_start(out=tile_sb[c][:, j : j + step, :], in_=pass_rows(dram, c)[:, j : j + step, :])
+        def load(tile_sb, dram, c, first, count):
+            nc.sync.dma_start(
+                out=tile_sb[c][:, first : first + count, :], in_=pass_rows(dram, c)[:, first : first + count, :]
+            )
 
-        def load_dy_inputs(c, pieces):
-            step = PACK // pieces
-            for j in range(0, PACK, step):
-                nc.sync.dma_start(out=g_sb[c][:, j : j + step, :], in_=pass_rows(grad_out, c)[:, j : j + step, :])
-                nc.sync.dma_start(out=p_sb[c][:, j : j + step, :], in_=pass_rows(p, c)[:, j : j + step, :])
-
-        load_dy_inputs(0, 2)
-        load(adj_sb, adj1, 0, 2)
+        for first, count in ((0, 1), (1, 1), (2, 2)):
+            load(g_sb, grad_out, 0, first, count)
+            load(p_sb, p, 0, first, count)
         for c in range(PASSES):
+            if c > 0:
+                load(g_sb, grad_out, c, 0, PACK)
+                load(p_sb, p, c, 0, 2)
+                load(p_sb, p, c, 2, 2)
+            adj_step = 1 if c == LAST else 2
+            for first in range(0, PACK, adj_step):
+                load(adj_sb, adj1, c, first, adj_step)
+            load(x_sb, x_gc2, c, 0, PACK)
             if c < LAST:
-                load_dy_inputs(c + 1, 1)
-            load(x_sb, x_gc2, c, 1)
-            if c < LAST:
-                load(nbar_sb, nbar, c, 1)
-                load(adj_sb, adj1, c + 1, 2)
-        piece_cols = FEAT // LAST_NBAR_PIECES
-        for w in range(0, FEAT, piece_cols):
-            nc.sync.dma_start(out=nbar_sb[LAST][:, :, w : w + piece_cols], in_=pass_rows(nbar, LAST)[:, :, w : w + piece_cols])
+                load(nbar_sb, nbar, c, 0, 2)
+                load(nbar_sb, nbar, c, 2, 2)
+        w = 0
+        for cols in LAST_NBAR_PIECES:
+            nc.sync.dma_start(out=nbar_sb[LAST][:, :, w : w + cols], in_=pass_rows(nbar, LAST)[:, :, w : w + cols])
+            w += cols
 
         def sum_grad_rows(c):
             for j in range(PACK):
@@ -115,37 +119,34 @@ def tile_gcn_pc_v_kernel(tc, x_gc2, adj1, W3, b3, nbar, p, grad_out, out):
             return fold
 
         def sum_adj_rows(c, fold):
-            for j in range(PACK):
-                if j == FOLDED_DEG_ROW:
-                    fold_copy = scrap.tile([P, FOLD_COLS], BF16, tag="fold_copy")
-                    nc.scalar.activation(
-                        out=fold_copy[:], in_=fold[:], func=ACT.Copy,
-                        accum_out=deg[c][:, j, 0:1],
-                    )
-                elif j == SCALAR_DEG_ROW:
-                    adj_copy_s = scrap.tile([P, NODES], BF16, tag="adj_copy_s")
-                    nc.scalar.activation(
-                        out=adj_copy_s[:], in_=adj_sb[c][:, j, :], func=ACT.Copy,
-                        accum_out=deg[c][:, j, 0:1],
-                    )
-                else:
-                    adj_copy_v = scrap.tile([P, NODES], BF16, tag="adj_copy_v")
-                    nc.vector.tensor_scalar(
-                        out=adj_copy_v[:], in0=adj_sb[c][:, j, :], scalar1=1.0, scalar2=None,
-                        op0=ALU.mult, op1=ALU.add, accum_out=deg[c][:, j, 0:1],
-                    )
+            for j in SCALAR_DEG_ROWS:
+                adj_copy_s = scrap.tile([P, NODES], BF16, tag="adj_copy_s")
+                nc.scalar.activation(
+                    out=adj_copy_s[:], in_=adj_sb[c][:, j, :], func=ACT.Copy,
+                    accum_out=deg[c][:, j, 0:1],
+                )
+            fold_copy = scrap.tile([P, FOLD_COLS], BF16, tag="fold_copy")
+            nc.scalar.activation(
+                out=fold_copy[:], in_=fold[:], func=ACT.Copy,
+                accum_out=deg[c][:, FOLDED_DEG_ROW, 0:1],
+            )
+            adj_copy_v = scrap.tile([P, NODES], BF16, tag="adj_copy_v")
+            nc.vector.tensor_scalar(
+                out=adj_copy_v[:], in0=adj_sb[c][:, VECTOR_DEG_ROW, :], scalar1=1.0, scalar2=None,
+                op0=ALU.mult, op1=ALU.add, accum_out=deg[c][:, VECTOR_DEG_ROW, 0:1],
+            )
 
-        def x_rows_of(c):
-            x_rows = work.tile([P, PACK, FEAT], BF16, tag="x_rows")
+        def x_rows_of(c, w, cols):
+            x_rows = work.tile([P, PACK, cols], BF16, tag="x_rows")
             for j in range(PACK):
                 nc.vector.tensor_scalar(
-                    out=x_rows[:, j, :], in0=x_sb[c][:, j, :], scalar1=deg[c][:, j, 0:1], scalar2=None,
+                    out=x_rows[:, j, :], in0=x_sb[c][:, j, w : w + cols], scalar1=deg[c][:, j, 0:1], scalar2=None,
                     op0=ALU.mult,
                 )
             return x_rows
 
-        def nbar_rows_of(c, w, cols):
-            n_rows = work.tile([P, PACK, cols], BF16, tag="n_rows")
+        def nbar_rows_of(c, w, cols, tag):
+            n_rows = work.tile([P, PACK, cols], BF16, tag=tag)
             for j in range(PACK):
                 nc.scalar.activation(
                     out=n_rows[:, j, :], in_=nbar_sb[c][:, j, w : w + cols], func=ACT.Copy,
@@ -153,9 +154,9 @@ def tile_gcn_pc_v_kernel(tc, x_gc2, adj1, W3, b3, nbar, p, grad_out, out):
                 )
             return n_rows
 
-        def regroup(rows, cols, tag, engine_copy):
+        def regroup(rows, cols, tag):
             grouped = work.tile([P, cols, PACK], BF16, tag=tag, align_bytes=64)
-            engine_copy(
+            nc.vector.tensor_copy(
                 out=grouped[:].rearrange("p (c i) j -> p c j i", i=RUN),
                 in_=rows[:].rearrange("p j (c i) -> p c j i", i=RUN),
             )
@@ -167,6 +168,21 @@ def tile_gcn_pc_v_kernel(tc, x_gc2, adj1, W3, b3, nbar, p, grad_out, out):
                 in_=grouped[:].rearrange("p w j -> p (w j)"),
             )
 
+        def multiply_waiting():
+            held = [one for one in waiting if one[1] >= len(acc)]
+            for c, t, codes, scales in [one for one in waiting if one[1] < len(acc)]:
+                nc.tensor.matmul_mx(
+                    out=acc[t][:],
+                    lhsT=codes.bitcast(E4M3_X4),
+                    lhsT_scale=scales,
+                    rhs=dy_codes[c][:].bitcast(E5M2_X4),
+                    rhs_scale=dy_scales[c][:],
+                    start=(c == 0),
+                    stop=(c == LAST),
+                )
+            waiting.clear()
+            waiting.extend(held)
+
         def quantise_m_and_multiply(c, grouped, first_row, cols):
             m_codes = packed.tile([P, cols], U32, name="m_codes%d_%d" % (c, first_row), align_bytes=64)
             m_scales = packed.tile([P, cols], U8, name="m_scales%d_%d" % (c, first_row), align_bytes=64)
@@ -176,57 +192,54 @@ def tile_gcn_pc_v_kernel(tc, x_gc2, adj1, W3, b3, nbar, p, grad_out, out):
             )
             for w in range(0, cols, M_TILE):
                 waiting.append((c, (first_row + w) // M_TILE, m_codes[:, w : w + M_TILE], m_scales[:, w : w + M_TILE]))
-            held = [one for one in waiting if one[1] >= len(acc)]
-            for c_of, t, codes, scales in [one for one in waiting if one[1] < len(acc)]:
-                nc.tensor.matmul_mx(
-                    out=acc[t][:],
-                    lhsT=codes.bitcast(E4M3_X4),
-                    lhsT_scale=scales,
-                    rhs=dy_codes[c_of][:].bitcast(E5M2_X4),
-                    rhs_scale=dy_scales[c_of][:],
-                    start=(c_of == 0),
-                    stop=(c_of == LAST),
-                )
-            waiting.clear()
-            waiting.extend(held)
+            multiply_waiting()
 
         def store(t, engine_copy):
             out_sb = results.tile([M_TILE, FEAT], F32, name="out_sb%d" % t)
             engine_copy(out=out_sb[:], in_=acc[t][:])
             nc.sync.dma_start(out=out[t * M_TILE : (t + 1) * M_TILE, :], in_=out_sb[:])
 
-        sum_grad_rows(0)
-        dy_rows = dy_rows_of(0)
-        dy_grouped = regroup(dy_rows, FEAT, "dy_grouped", nc.vector.tensor_copy)
-        sum_adj_rows(0, fold_adj_row(0))
-        quantise_dy(0, dy_grouped)
-        for c in range(LAST):
-            fold = fold_adj_row(c + 1)
-            sum_grad_rows(c + 1)
-            dy_rows = dy_rows_of(c + 1)
-            x_rows = x_rows_of(c)
-            n_rows = nbar_rows_of(c, 0, FEAT)
-            dy_grouped = regroup(dy_rows, FEAT, "dy_grouped", nc.vector.tensor_copy)
-            x_grouped = regroup(x_rows, FEAT, "x_grouped", nc.vector.tensor_copy)
-            n_grouped = regroup(n_rows, FEAT, "n_grouped", nc.scalar.copy)
-            quantise_dy(c + 1, dy_grouped)
-            quantise_m_and_multiply(c, x_grouped, 0, FEAT)
-            sum_adj_rows(c + 1, fold)
-            if c + 1 == LAST:
-                acc.append(psum.tile([M_TILE, FEAT], F32, name="acc%d" % LENT_TILE, tag="lent_bank"))
-            quantise_m_and_multiply(c, n_grouped, FEAT, FEAT)
+        n_grouped = None
+        for c in range(PASSES):
+            sum_grad_rows(c)
+            dy_rows = dy_rows_of(c)
+            fold = fold_adj_row(c)
+            dy_grouped = regroup(dy_rows, FEAT, "dy_grouped")
+            if c > 0:
+                quantise_m_and_multiply(c - 1, n_grouped, FEAT, FEAT)
+            quantise_dy(c, dy_grouped)
+            sum_adj_rows(c, fold)
+            if c < LAST:
+                x_rows = x_rows_of(c, 0, FEAT)
+                x_grouped = regroup(x_rows, FEAT, "x_grouped")
+                n_rows = nbar_rows_of(c, 0, FEAT, "n_rows")
+                quantise_m_and_multiply(c, x_grouped, 0, FEAT)
+                n_grouped = regroup(n_rows, FEAT, "n_grouped")
+        acc.append(psum.tile([M_TILE, FEAT], F32, name="acc%d" % LENT_TILE, tag="lent_bank"))
+        multiply_waiting()
 
-        x_rows = x_rows_of(LAST)
-        n_rows = [nbar_rows_of(LAST, w, piece_cols) for w in range(0, FEAT, piece_cols)]
-        x_grouped = regroup(x_rows, FEAT, "x_grouped", nc.vector.tensor_copy)
-        n_grouped = regroup(n_rows[0], piece_cols, "n_grouped", nc.vector.tensor_copy)
-        quantise_m_and_multiply(LAST, x_grouped, 0, FEAT)
-        for t in range(FEAT // M_TILE):
-            store(t, nc.scalar.copy)
-        for k in range(LAST_NBAR_PIECES):
-            this_grouped = n_grouped
-            if k + 1 < LAST_NBAR_PIECES:
-                n_grouped = regroup(n_rows[k + 1], piece_cols, "n_grouped", nc.vector.tensor_copy)
-            quantise_m_and_multiply(LAST, this_grouped, FEAT + k * piece_cols, piece_cols)
-        for t in range(FEAT // M_TILE, 2 * FEAT // M_TILE):
-            store(t, nc.scalar.copy if t % 2 == 0 else nc.vector.tensor_copy)
+        xa_rows = x_rows_of(LAST, 0, 256)
+        xa_grouped = regroup(xa_rows, 256, "x_grouped")
+        xb_rows = x_rows_of(LAST, 256, 256)
+        quantise_m_and_multiply(LAST, xa_grouped, 0, 256)
+        xb_grouped = regroup(xb_rows, 256, "x_grouped")
+        n_pieces = []
+        w = 0
+        for cols in LAST_NBAR_PIECES:
+            n_pieces.append(nbar_rows_of(LAST, w, cols, "n_piece%d" % w))
+            w += cols
+        store(0, nc.vector.tensor_copy)
+        quantise_m_and_multiply(LAST, xb_grouped, 256, 256)
+        store(1, nc.vector.tensor_copy)
+        n0_grouped = regroup(n_pieces[0], 256, "n_grouped")
+        n1_grouped = regroup(n_pieces[1], 128, "n_grouped")
+        quantise_m_and_multiply(LAST, n0_grouped, FEAT, 256)
+        store(2, nc.scalar.copy)
+        store(3, nc.scalar.copy)
+        n2_grouped = regroup(n_pieces[2], 128, "n_grouped")
+        quantise_m_and_multiply(LAST, n1_grouped, FEAT + 256, 128)
+        quantise_m_and_multiply(LAST, n2_grouped, FEAT + 384, 128)
+        store(4, nc.scalar.copy)
+        store(5, nc.vector.tensor_copy)
+        store(6, nc.scalar.copy)
+        store(7, nc.vector.tensor_copy)

@@ -21,7 +21,7 @@ LAST = PASSES - 1
 FEAT = 512
 M_TILE = 128
 TILES = 2 * FEAT // M_TILE
-RUN = 4
+RUN = 8
 SUM_PITCH = 8
 FOLD_COLS = 128
 SCALAR_DEG_ROWS = (0, 1)

@@ -22,6 +22,7 @@ FEAT = 512
 M_TILE = 128
 TILES = 2 * FEAT // M_TILE
 RUN = 8
+N_RUN = 4
 SUM_PITCH = 8
 FOLD_COLS = 128
 SCALAR_DEG_ROWS = (0, 1)
@@ -154,6 +155,16 @@ def tile_gcn_pc_v_kernel(tc, x_gc2, adj1, W3, b3, nbar, p, grad_out, out):
                 )
             return n_rows
 
+        def nbar_grouped_of(c, w, cols, tag):
+            grouped = work.tile([P, cols, PACK], BF16, tag=tag, align_bytes=64)
+            nc.vector.tensor_tensor(
+                out=grouped[:].rearrange("p (c i) j -> p c j i", i=N_RUN),
+                in0=nbar_sb[c][:, :, w : w + cols].rearrange("p j (c i) -> p c j i", i=N_RUN),
+                in1=deg[c][:, :, 0:1].unsqueeze(1).to_broadcast([P, cols // N_RUN, PACK, N_RUN]),
+                op=ALU.mult,
+            )
+            return grouped
+
         def regroup(rows, cols, tag):
             grouped = work.tile([P, cols, PACK], BF16, tag=tag, align_bytes=64)
             nc.vector.tensor_copy(
@@ -223,20 +234,16 @@ def tile_gcn_pc_v_kernel(tc, x_gc2, adj1, W3, b3, nbar, p, grad_out, out):
         xb_rows = x_rows_of(LAST, 256, 256)
         quantise_m_and_multiply(LAST, xa_grouped, 0, 256)
         xb_grouped = regroup(xb_rows, 256, "x_grouped")
-        n_pieces = []
-        w = 0
-        for cols in LAST_NBAR_PIECES:
-            n_pieces.append(nbar_rows_of(LAST, w, cols, "n_piece%d" % w))
-            w += cols
-        store(0, nc.vector.tensor_copy)
+        n0_rows = nbar_rows_of(LAST, 0, 256, "n_piece0")
+        store(0, nc.scalar.copy)
         quantise_m_and_multiply(LAST, xb_grouped, 256, 256)
-        store(1, nc.vector.tensor_copy)
-        n0_grouped = regroup(n_pieces[0], 256, "n_grouped")
-        n1_grouped = regroup(n_pieces[1], 128, "n_grouped")
+        store(1, nc.scalar.copy)
+        n0_grouped = regroup(n0_rows, 256, "n_grouped")
+        n1_grouped = nbar_grouped_of(LAST, 256, 128, "n_grouped")
         quantise_m_and_multiply(LAST, n0_grouped, FEAT, 256)
         store(2, nc.scalar.copy)
         store(3, nc.scalar.copy)
-        n2_grouped = regroup(n_pieces[2], 128, "n_grouped")
+        n2_grouped = nbar_grouped_of(LAST, 384, 128, "n_grouped")
         quantise_m_and_multiply(LAST, n1_grouped, FEAT + 256, 128)
         quantise_m_and_multiply(LAST, n2_grouped, FEAT + 384, 128)
         store(4, nc.scalar.copy)

from contextlib import ExitStack

import concourse.mybir as mybir
from concourse.masks import make_identity

F32 = mybir.dt.float32
BF16 = mybir.dt.bfloat16
U32 = mybir.dt.uint32
U8 = mybir.dt.uint8
E4M3_X4 = mybir.dt.float8_e4m3fn_x4
E5M2_X4 = mybir.dt.float8_e5m2_x4
ALU = mybir.AluOpType
ACT = mybir.ActivationFunctionType

P = 128
PACK = 4
K_PASS = P * PACK
NODES = 1536
PASSES = NODES // K_PASS
LAST = PASSES - 1
FEAT = 512
M_TILE = 128
TILES = 2 * FEAT // M_TILE
RUN = 8
N_RUN = 4
SUM_PITCH = 8
FOLD_COLS = 128
SCALAR_DEG_ROWS = (0, 1)
FOLDED_DEG_ROW = 2
VECTOR_DEG_ROW = 3
LENT_TILE = TILES - 1
LAST_X_PIECES = (256, 256)
LAST_NBAR_PIECES = (256, 128, 128)

FLOPS = 2 * NODES * (2 * FEAT) * FEAT
BYTES = NODES * NODES * 2 + 2 * NODES * FEAT * 2 + 2 * NODES * FEAT * 4 + 2 * FEAT * FEAT * 4


def pass_rows(dram, c):
    return dram[c * K_PASS : (c + 1) * K_PASS, :].rearrange("(p j) w -> p j w", j=PACK)


def tile_gcn_pc_v_kernel(tc, x_gc2, adj1, W3, b3, nbar, p, grad_out, out):
    nc = tc.nc
    with ExitStack() as ctx:
        inputs = ctx.enter_context(tc.tile_pool(name="inputs", bufs=1))
        sums = ctx.enter_context(tc.tile_pool(name="sums", bufs=1))
        scrap = ctx.enter_context(tc.tile_pool(name="scrap", bufs=2))
        work = ctx.enter_context(tc.tile_pool(name="work", bufs=2))
        packed = ctx.enter_context(tc.tile_pool(name="packed", bufs=1))
        results = ctx.enter_context(tc.tile_pool(name="results", bufs=1))
        psum = ctx.enter_context(tc.psum_pool(name="psum", bufs=1))
        ctx.enter_context(tc.manual_schedule())

        g_sb = [inputs.tile([P, PACK, FEAT], BF16, name="g%d" % c) for c in range(PASSES)]
        p_sb = [inputs.tile([P, PACK, FEAT], F32, name="p%d" % c) for c in range(PASSES)]
        adj_sb = [inputs.tile([P, PACK, NODES], BF16, name="adj%d" % c) for c in range(PASSES)]
        x_sb = [inputs.tile([P, PACK, FEAT], BF16, name="x%d" % c) for c in range(PASSES)]
        nbar_sb = [inputs.tile([P, PACK, FEAT], F32, name="nbar%d" % c) for c in range(PASSES)]
        neg_gsum = [sums.tile([P, PACK, SUM_PITCH], F32, name="neg_gsum%d" % c) for c in range(PASSES)]
        deg = [sums.tile([P, PACK, SUM_PITCH], F32, name="deg%d" % c) for c in range(PASSES)]
        dy_codes = [packed.tile([P, FEAT], U32, name="dy_codes%d" % c, align_bytes=64) for c in range(PASSES)]
        dy_scales = [packed.tile([P, FEAT], U8, name="dy_scales%d" % c, align_bytes=64) for c in range(PASSES)]
        acc = [psum.tile([M_TILE, FEAT], F32, name="acc%d" % t) for t in range(LENT_TILE)]
        waiting = []
        ident = sums.tile([P, P], BF16, name="ident")
        make_identity(nc, ident[:])

        def load(tile_sb, dram, c, first, count):
            nc.sync.dma_start(
                out=tile_sb[c][:, first : first + count, :], in_=pass_rows(dram, c)[:, first : first + count, :]
            )

        for first, count in ((0, 1), (1, 1), (2, 2)):
            load(g_sb, grad_out, 0, first, count)
            load(p_sb, p, 0, first, count)
        for c in range(PASSES):
            if c > 0:
                load(g_sb, grad_out, c, 0, PACK)
                load(p_sb, p, c, 0, 2)
                load(p_sb, p, c, 2, 2)
            adj_step = 1 if c == LAST else 2
            for first in range(0, PACK, adj_step):
                load(adj_sb, adj1, c, first, adj_step)
            load(x_sb, x_gc2, c, 0, PACK)
            if c < LAST:
                load(nbar_sb, nbar, c, 0, 2)
                load(nbar_sb, nbar, c, 2, 2)
        w = 0
        for cols in LAST_NBAR_PIECES:
            nc.sync.dma_start(out=nbar_sb[LAST][:, :, w : w + cols], in_=pass_rows(nbar, LAST)[:, :, w : w + cols])
            w += cols

        def sum_grad_rows(c):
            for j in range(PACK):
                neg_g = scrap.tile([P, FEAT], BF16, tag="neg_g")
                nc.scalar.activation(
                    out=neg_g[:], in_=g_sb[c][:, j, :], func=ACT.Copy, scale=-1.0,
                    accum_out=neg_gsum[c][:, j, 0:1],
                )

        def dy_rows_of(c):
            dy_rows = work.tile([P, PACK, FEAT], BF16, tag="dy_rows")
            for j in range(PACK):
                nc.vector.scalar_tensor_tensor(
                    out=dy_rows[:, j, :], in0=p_sb[c][:, j, :], scalar=neg_gsum[c][:, j, 0:1],
                    in1=g_sb[c][:, j, :], op0=ALU.mult, op1=ALU.add,
                )
            return dy_rows

        def fold_adj_row(c):
            fold = psum.tile([P, FOLD_COLS], F32, name="fold%d" % c, tag="lent_bank")
            pieces = NODES // FOLD_COLS
            for k in range(pieces):
                nc.tensor.matmul(
                    out=fold[:], lhsT=ident[:],
                    rhs=adj_sb[c][:, FOLDED_DEG_ROW, k * FOLD_COLS : (k + 1) * FOLD_COLS],
                    start=(k == 0), stop=(k == pieces - 1),
                )
            return fold

        def sum_adj_rows(c, fold):
            for j in SCALAR_DEG_ROWS:
                adj_copy_s = scrap.tile([P, NODES], BF16, tag="adj_copy_s")
                nc.scalar.activation(
                    out=adj_copy_s[:], in_=adj_sb[c][:, j, :], func=ACT.Copy,
                    accum_out=deg[c][:, j, 0:1],
                )
            fold_copy = scrap.tile([P, FOLD_COLS], BF16, tag="fold_copy")
            nc.scalar.activation(
                out=fold_copy[:], in_=fold[:], func=ACT.Copy,
                accum_out=deg[c][:, FOLDED_DEG_ROW, 0:1],
            )
            adj_copy_v = scrap.tile([P, NODES], BF16, tag="adj_copy_v")
            nc.vector.tensor_scalar(
                out=adj_copy_v[:], in0=adj_sb[c][:, VECTOR_DEG_ROW, :], scalar1=1.0, scalar2=None,
                op0=ALU.mult, op1=ALU.add, accum_out=deg[c][:, VECTOR_DEG_ROW, 0:1],
            )

        def x_rows_of(c, w, cols):
            x_rows = work.tile([P, PACK, cols], BF16, tag="x_rows")
            for j in range(PACK):
                nc.vector.tensor_scalar(
                    out=x_rows[:, j, :], in0=x_sb[c][:, j, w : w + cols], scalar1=deg[c][:, j, 0:1], scalar2=None,
                    op0=ALU.mult,
                )
            return x_rows

        def nbar_rows_of(c, w, cols, tag):
            n_rows = work.tile([P, PACK, cols], BF16, tag=tag)
            for j in range(PACK):
                nc.scalar.activation(
                    out=n_rows[:, j, :], in_=nbar_sb[c][:, j, w : w + cols], func=ACT.Copy,
                    scale=deg[c][:, j, 0:1],
                )
            return n_rows

        def nbar_grouped_of(c, w, cols, tag):
            grouped = work.tile([P, cols, PACK], BF16, tag=tag, align_bytes=64)
            nc.vector.tensor_tensor(
                out=grouped[:].rearrange("p (c i) j -> p c j i", i=N_RUN),
                in0=nbar_sb[c][:, :, w : w + cols].rearrange("p j (c i) -> p c j i", i=N_RUN),
                in1=deg[c][:, :, 0:1].unsqueeze(1).to_broadcast([P, cols // N_RUN, PACK, N_RUN]),
                op=ALU.mult,
            )
            return grouped

        def regroup(rows, cols, tag):
            grouped = work.tile([P, cols, PACK], BF16, tag=tag, align_bytes=64)
            nc.vector.tensor_copy(
                out=grouped[:].rearrange("p (c i) j -> p c j i", i=RUN),
                in_=rows[:].rearrange("p j (c i) -> p c j i", i=RUN),
            )
            return grouped

        def quantise_dy(c, grouped):
            nc.vector.quantize_mx(
                out=dy_codes[c][:].bitcast(E5M2_X4), scales=dy_scales[c][:],
                in_=grouped[:].rearrange("p w j -> p (w j)"),
            )

        def multiply_waiting():
            held = [one for one in waiting if one[1] >= len(acc)]
            for c, t, codes, scales in [one for one in waiting if one[1] < len(acc)]:
                nc.tensor.matmul_mx(
                    out=acc[t][:],
                    lhsT=codes.bitcast(E4M3_X4),
                    lhsT_scale=scales,
                    rhs=dy_codes[c][:].bitcast(E5M2_X4),
                    rhs_scale=dy_scales[c][:],
                    start=(c == 0),
                    stop=(c == LAST),
                )
            waiting.clear()
            waiting.extend(held)

        def quantise_m_and_multiply(c, grouped, first_row, cols):
            m_codes = packed.tile([P, cols], U32, name="m_codes%d_%d" % (c, first_row), align_bytes=64)
            m_scales = packed.tile([P, cols], U8, name="m_scales%d_%d" % (c, first_row), align_bytes=64)
            nc.vector.quantize_mx(
                out=m_codes[:].bitcast(E4M3_X4), scales=m_scales[:],
                in_=grouped[:].rearrange("p w j -> p (w j)"),
            )
            for w in range(0, cols, M_TILE):
                waiting.append((c, (first_row + w) // M_TILE, m_codes[:, w : w + M_TILE], m_scales[:, w : w + M_TILE]))
            multiply_waiting()

        def store(t, engine_copy):
            out_sb = results.tile([M_TILE, FEAT], F32, name="out_sb%d" % t)
            engine_copy(out=out_sb[:], in_=acc[t][:])
            nc.sync.dma_start(out=out[t * M_TILE : (t + 1) * M_TILE, :], in_=out_sb[:])

        n_grouped = None
        for c in range(PASSES):
            sum_grad_rows(c)
            dy_rows = dy_rows_of(c)
            fold = fold_adj_row(c)
            dy_grouped = regroup(dy_rows, FEAT, "dy_grouped")
            if c > 0:
                quantise_m_and_multiply(c - 1, n_grouped, FEAT, FEAT)
            quantise_dy(c, dy_grouped)
            sum_adj_rows(c, fold)
            if c < LAST:
                x_rows = x_rows_of(c, 0, FEAT)
                x_grouped = regroup(x_rows, FEAT, "x_grouped")
                n_rows = nbar_rows_of(c, 0, FEAT, "n_rows")
                quantise_m_and_multiply(c, x_grouped, 0, FEAT)
                n_grouped = regroup(n_rows, FEAT, "n_grouped")
        acc.append(psum.tile([M_TILE, FEAT], F32, name="acc%d" % LENT_TILE, tag="lent_bank"))
        multiply_waiting()

        xa_rows = x_rows_of(LAST, 0, 256)
        xa_grouped = regroup(xa_rows, 256, "x_grouped")
        xb_rows = x_rows_of(LAST, 256, 256)
        quantise_m_and_multiply(LAST, xa_grouped, 0, 256)
        xb_grouped = regroup(xb_rows, 256, "x_grouped")
        n0_rows = nbar_rows_of(LAST, 0, 256, "n_piece0")
        store(0, nc.scalar.copy)
        quantise_m_and_multiply(LAST, xb_grouped, 256, 256)
        store(1, nc.scalar.copy)
        n0_grouped = regroup(n0_rows, 256, "n_grouped")
        n1_grouped = nbar_grouped_of(LAST, 256, 128, "n_grouped")
        quantise_m_and_multiply(LAST, n0_grouped, FEAT, 256)
        store(2, nc.scalar.copy)
        store(3, nc.scalar.copy)
        n2_grouped = nbar_grouped_of(LAST, 384, 128, "n_grouped")
        quantise_m_and_multiply(LAST, n1_grouped, FEAT + 256, 128)
        quantise_m_and_multiply(LAST, n2_grouped, FEAT + 384, 128)
        store(4, nc.scalar.copy)
        store(5, nc.vector.tensor_copy)
        store(6, nc.scalar.copy)
        store(7, nc.vector.tensor_copy)
